import numpy as np
import ml_dtypes


def mxq(x, axis, fmt="e4m3"):
    dtype, down = {"e4m3": (ml_dtypes.float8_e4m3fn, 7), "e5m2": (ml_dtypes.float8_e5m2, 14)}[fmt]
    v = np.moveaxis(np.asarray(x, np.float32).astype(ml_dtypes.bfloat16).astype(np.float64), axis, -1)
    blocks = v.reshape(v.shape[:-1] + (-1, 32))
    amax = np.abs(blocks).max(-1, keepdims=True)
    byte = np.maximum(np.where(amax > 0, np.frexp(amax)[1] - 1 + 127, 0) - down, 1)
    scale = np.exp2(byte - 127.0)
    codes = (blocks / scale).astype(np.float32).astype(dtype).astype(np.float64)
    return np.moveaxis((codes * scale).reshape(v.shape), -1, axis)


WIDE = False


def mx_kscale(k):
    if not WIDE:
        return np.ones(k)
    levels = np.array([10, -10, 5, -5, 0])
    a = np.random.permutation(np.resize(levels, k // 512 * 4)).reshape(k // 512, 4)
    idx = np.arange(k)
    return np.exp2(a[idx // 512, idx % 128 // 32])


BF16 = ml_dtypes.bfloat16


def bf(x):
    return np.asarray(x, np.float32).astype(BF16)


def f64(x):
    return np.asarray(x).astype(np.float64)


B, N, D, H, DH = 2, 512, 1024, 8, 128
E = H * DH
GAIN = np.sqrt(1.8 / DH)


def setup_inputs():
    t = mx_kscale(E)
    return {"q_rot": bf(np.random.standard_normal((B, H, N, DH)) * GAIN),
            "k_rot": bf(np.random.standard_normal((B, H, N, DH)) * GAIN),
            "v": bf(np.random.standard_normal((B, H, N, DH)) * t.reshape(H, 1, DH)),
            "w_out": bf(np.random.standard_normal((E, D)) * E ** -0.5 / t[:, None]),
            "b_out": bf(np.random.standard_normal(D) * 0.2)}


def reference(q_rot, k_rot, v, w_out, b_out):
    scores = f64(q_rot) @ f64(k_rot).transpose(0, 1, 3, 2) * np.sqrt(DH)
    e = np.exp(scores - scores.max(-1, keepdims=True))
    p = e / e.sum(-1, keepdims=True)
    gate = p.sum(axis=2)
    attn = f64(v) * gate[..., None]
    attn = attn.transpose(0, 2, 1, 3).reshape(B, N, E)
    return (mxq(attn, 2, "e4m3") @ mxq(f64(w_out), 0, "e4m3")) + f64(b_out)

@@ -1,0 +1,213 @@
+from contextlib import ExitStack
+import math
+
+import concourse.bass as bass
+import concourse.masks as masks
+import concourse.mybir as mybir
+import concourse.tile as tile
+
+BF16 = mybir.dt.bfloat16
+F32 = mybir.dt.float32
+U32 = mybir.dt.uint32
+U8 = mybir.dt.uint8
+FP8X4 = mybir.dt.float8_e4m3fn_x4
+ACT = mybir.ActivationFunctionType
+ALU = mybir.AluOpType
+AX = mybir.AxisListType
+
+P = 128
+B, H, N, DH, D = 2, 8, 512, 128, 1024
+NH = B * H
+NC = N // P
+SCALE = math.sqrt(DH)
+FLOPS = 2 * NH * N * N * DH + 2 * NH * N * N + 2 * B * N * H * DH * D
+
+
+def tile_attn_pb_kernel(tc, q_rot, k_rot, v, w_out, b_out, out):
+    nc = tc.nc
+    with ExitStack() as ctx:
+        const = ctx.enter_context(tc.tile_pool(name="const", bufs=1))
+        keep = ctx.enter_context(tc.tile_pool(name="keep", bufs=1))
+        qk_pool = ctx.enter_context(tc.tile_pool(name="qkt", bufs=3))
+        e_pool = ctx.enter_context(tc.tile_pool(name="e", bufs=4))
+        st_pool = ctx.enter_context(tc.tile_pool(name="stat", bufs=4))
+        a_pool = ctx.enter_context(tc.tile_pool(name="a", bufs=2))
+        o_pool = ctx.enter_context(tc.tile_pool(name="o", bufs=3))
+        ps_s = ctx.enter_context(tc.psum_pool(name="ps_s", bufs=4))
+        ps_t = ctx.enter_context(tc.psum_pool(name="ps_t", bufs=1))
+        ps_c = ctx.enter_context(tc.psum_pool(name="ps_c", bufs=1))
+        ps_o = ctx.enter_context(tc.psum_pool(name="ps_o", bufs=2))
+
+        ident = const.tile([P, P], BF16, name="ident")
+        masks.make_identity(nc, ident[:])
+        ident_f = const.tile([P, P], F32, name="ident_f")
+        masks.make_identity(nc, ident_f[:])
+
+        qv = q_rot.rearrange("b h (p c) d -> p (b h) (c d)", c=NC)
+        kv = k_rot.rearrange("b h (p c) d -> p (b h) (c d)", c=NC)
+        vv = v.rearrange("b h (p c) d -> p (b h) (c d)", c=NC)
+        wv = w_out.rearrange("(g t p) n -> p g t n", g=2, t=4)
+        q_sb, k_sb, v_sb = [], [], []
+        for i in range(NH // 2):
+            q_sb.append(keep.tile([P, 2, N], BF16, name="q%d" % i))
+            k_sb.append(keep.tile([P, 2, N], BF16, name="k%d" % i))
+            v_sb.append(keep.tile([P, 2, N], BF16, name="v%d" % i))
+        w_raw = [keep.tile([P, 4, D], BF16, name="wraw%d" % g) for g in range(2)]
+        bias_bc = keep.tile([P, D], BF16, name="bias_bc")
+
+        def load_pair(i):
+            nc.sync.dma_start(out=q_sb[i][:], in_=qv[:, 2 * i:2 * i + 2, :])
+            nc.sync.dma_start(out=k_sb[i][:], in_=kv[:, 2 * i:2 * i + 2, :])
+            nc.sync.dma_start(out=v_sb[i][:], in_=vv[:, 2 * i:2 * i + 2, :])
+
+        load_pair(0)
+        load_pair(1)
+        nc.sync.dma_start(out=w_raw[0][:], in_=wv[:, 0])
+        load_pair(2)
+        nc.sync.dma_start(out=w_raw[1][:], in_=wv[:, 1])
+        load_pair(3)
+        nc.sync.dma_start(out=bias_bc[:], in_=b_out.partition_broadcast(P))
+        for i in range(4, NH // 2):
+            load_pair(i)
+
+        w_grp = [keep.tile([P, D, 4], BF16, name="wgrp%d" % g, align_bytes=64) for g in range(2)]
+        w_codes = keep.tile([P, 2, D], U32, name="w_codes", align_bytes=64)
+        w_scales = keep.tile([P, 2, D], U8, name="w_scales", align_bytes=64)
+
+        def w_regroup(g, piece):
+            cols = slice(piece * 256, (piece + 1) * 256)
+            nc.vector.tensor_copy(
+                out=w_grp[g][:, cols, :].rearrange("p (c i) t -> p c t i", i=4),
+                in_=w_raw[g][:, :, cols].rearrange("p t (c i) -> p c t i", i=4),
+            )
+
+        def w_quant(g, half):
+            cols = slice(half * 512, (half + 1) * 512)
+            nc.vector.quantize_mx(
+                out=w_codes[:, g, cols].bitcast(FP8X4),
+                scales=w_scales[:, g, cols],
+                in_=w_grp[g][:, cols, :].rearrange("p n t -> p (n t)"),
+            )
+
+        qkT = {}
+        e_sb = {}
+        rsum = {}
+        a4 = {}
+        a_codes = {}
+        a_scales = {}
+
+        def stage_t(i):
+            tp = ps_t.tile([P, 2 * N], BF16, name="tp", tag="t")
+            for c in range(NC):
+                nc.tensor.transpose(out=tp[:, c * P:(c + 1) * P],
+                                    in_=q_sb[i // 2][:, i % 2, c * P:(c + 1) * P], identity=ident[:])
+            for c in range(NC):
+                nc.tensor.transpose(out=tp[:, N + c * P:N + (c + 1) * P],
+                                    in_=k_sb[i // 2][:, i % 2, c * P:(c + 1) * P], identity=ident[:])
+            t_sb = qk_pool.tile([P, 2 * N], BF16, name="qkT")
+            nc.scalar.copy(out=t_sb[:], in_=tp[:])
+            qkT[i] = t_sb
+
+        def stage_s(i):
+            t_sb = qkT[i]
+            e_t = e_pool.tile([P, NC, N], F32, name="e_t")
+            mx = st_pool.tile([P, NC], F32, name="mx")
+            nb = st_pool.tile([P, NC], F32, name="nb")
+            rs = st_pool.tile([P, NC], F32, name="rs")
+            for pair in range(2):
+                banks = []
+                for c in (2 * pair, 2 * pair + 1):
+                    s_ps = ps_s.tile([P, N], F32, name="s_ps")
+                    nc.tensor.matmul(out=s_ps[:], lhsT=t_sb[:, c * P:(c + 1) * P], rhs=t_sb[:, N:2 * N],
+                                     start=True, stop=True)
+                    nc.vector.tensor_reduce(out=mx[:, c:c + 1], in_=s_ps[:], axis=AX.X, op=ALU.max)
+                    banks.append(s_ps)
+                two = slice(2 * pair, 2 * pair + 2)
+                nc.vector.tensor_scalar(out=nb[:, two], in0=mx[:, two], scalar1=-SCALE, scalar2=None,
+                                        op0=ALU.mult)
+                for c in (2 * pair, 2 * pair + 1):
+                    nc.scalar.activation(out=e_t[:, c, :], in_=banks[c % 2][:], func=ACT.Exp,
+                                         bias=nb[:, c:c + 1], scale=SCALE, accum_out=rs[:, c:c + 1])
+            e_sb[i] = e_t
+            rsum[i] = rs
+
+        def stage_r(i):
+            e_t = e_sb[i]
+            rr = st_pool.tile([P, NC], F32, name="rr")
+            nc.vector.reciprocal(out=rr[:], in_=rsum[i][:])
+            for c in range(NC):
+                nc.gpsimd.tensor_scalar(out=e_t[:, c, :], in0=e_t[:, c, :], scalar1=rr[:, c:c + 1],
+                                        scalar2=0.0, op0=ALU.mult, op1=ALU.add)
+
+        def stage_g(i):
+            bg, t = i // 4, i % 4
+            e_t = e_sb[i]
+            cg = ps_c.tile([P, NC, P], F32, name="cg")
+            for j in range(NC):
+                for c in range(NC):
+                    nc.tensor.matmul(out=cg[:, j, :], lhsT=e_t[:, c, j * P:(j + 1) * P], rhs=ident_f[:],
+                                     start=(c == 0), stop=(c == NC - 1), is_transpose=True)
+            cv = st_pool.tile([P, NC], F32, name="cv")
+            nc.vector.tensor_reduce(out=cv[:], in_=cg[:], axis=AX.X, op=ALU.add)
+            if t == 0:
+                a4[bg] = a_pool.tile([P, 4, NC, DH], BF16, name="a4")
+            for j in range(NC):
+                nc.vector.tensor_scalar(out=a4[bg][:, t, j, :],
+                                        in0=v_sb[i // 2][:, i % 2, j * P:(j + 1) * P],
+                                        scalar1=cv[:, j:j + 1], scalar2=None, op0=ALU.mult)
+
+        def stage_a(bg):
+            grp = a_pool.tile([P, 2, 2 * P, 4], BF16, name="grp", align_bytes=64)
+            for jj in range(2):
+                ta = ps_t.tile([P, 4, 2 * P], BF16, name="ta", tag="t")
+                for t in range(4):
+                    for jl in range(2):
+                        nc.tensor.transpose(out=ta[:, t, jl * P:(jl + 1) * P],
+                                            in_=a4[bg][:, t, 2 * jj + jl, :], identity=ident[:])
+                if jj == 0 or bg < 3:
+                    nc.scalar.copy(out=grp[:, jj, :, :], in_=ta[:].rearrange("p t x -> p x t"))
+                else:
+                    nc.vector.tensor_copy(out=grp[:, jj, :, :], in_=ta[:].rearrange("p t x -> p x t"))
+            a_codes[bg] = keep.tile([P, N], U32, name="a_codes%d" % bg, align_bytes=64)
+            a_scales[bg] = keep.tile([P, N], U8, name="a_scales%d" % bg, align_bytes=64)
+            nc.vector.quantize_mx(out=a_codes[bg][:].bitcast(FP8X4), scales=a_scales[bg][:],
+                                  in_=grp[:].rearrange("p a x t -> p (a x t)"))
+
+        ov = out.rearrange("b (p j) n -> b j p n", j=NC)
+
+        def stage_o(b):
+            for j in range(NC):
+                o_sb = o_pool.tile([P, D], F32, name="o_sb")
+                for nh in range(2):
+                    cols = slice(nh * 512, (nh + 1) * 512)
+                    o_ps = ps_o.tile([P, 512], F32, name="o_ps")
+                    for g in range(2):
+                        nc.tensor.matmul_mx(
+                            out=o_ps[:],
+                            lhsT=a_codes[2 * b + g][:, j * P:(j + 1) * P].bitcast(FP8X4),
+                            lhsT_scale=a_scales[2 * b + g][:, j * P:(j + 1) * P],
+                            rhs=w_codes[:, g, cols].bitcast(FP8X4),
+                            rhs_scale=w_scales[:, g, cols],
+                            start=(g == 0), stop=(g == 1))
+                    nc.vector.tensor_tensor(out=o_sb[:, cols], in0=o_ps[:], in1=bias_bc[:, cols], op=ALU.add)
+                nc.sync.dma_start(out=ov[b, j], in_=o_sb[:])
+
+        for step in range(NH + 3):
+            if step < NH:
+                stage_t(step)
+            if 1 <= step <= NH:
+                stage_s(step - 1)
+            if 2 <= step <= NH + 1:
+                stage_r(step - 2)
+            if 2 <= step <= 5:
+                g = (step - 2) // 2
+                for piece in range(2):
+                    w_regroup(g, 2 * ((step - 2) % 2) + piece)
+                w_quant(g, (step - 2) % 2)
+            if step >= 3:
+                i = step - 3
+                stage_g(i)
+                if i % 4 == 3:
+                    stage_a(i // 4)
+                if i % 8 == 7:
+                    stage_o(i // 8)

@@ -1,10 +1,8 @@
 from contextlib import ExitStack
 import math
 
-import concourse.bass as bass
 import concourse.masks as masks
 import concourse.mybir as mybir
-import concourse.tile as tile
 
 BF16 = mybir.dt.bfloat16
 F32 = mybir.dt.float32
@@ -19,6 +17,7 @@ P = 128
 B, H, N, DH, D = 2, 8, 512, 128, 1024
 NH = B * H
 NC = N // P
+NS = NH * NC
 SCALE = math.sqrt(DH)
 FLOPS = 2 * NH * N * N * DH + 2 * NH * N * N + 2 * B * N * H * DH * D
 
@@ -28,186 +27,259 @@ def tile_attn_pb_kernel(tc, q_rot, k_rot, v, w_out, b_out, out):
     with ExitStack() as ctx:
         const = ctx.enter_context(tc.tile_pool(name="const", bufs=1))
         keep = ctx.enter_context(tc.tile_pool(name="keep", bufs=1))
-        qk_pool = ctx.enter_context(tc.tile_pool(name="qkt", bufs=3))
-        e_pool = ctx.enter_context(tc.tile_pool(name="e", bufs=4))
-        st_pool = ctx.enter_context(tc.tile_pool(name="stat", bufs=4))
+        qk_pool = ctx.enter_context(tc.tile_pool(name="qkt", bufs=4))
+        e_pool = ctx.enter_context(tc.tile_pool(name="e", bufs=5))
+        st_pool = ctx.enter_context(tc.tile_pool(name="stat", bufs=6))
         a_pool = ctx.enter_context(tc.tile_pool(name="a", bufs=2))
-        o_pool = ctx.enter_context(tc.tile_pool(name="o", bufs=3))
+        o_pool = ctx.enter_context(tc.tile_pool(name="o", bufs=4))
         ps_s = ctx.enter_context(tc.psum_pool(name="ps_s", bufs=4))
         ps_t = ctx.enter_context(tc.psum_pool(name="ps_t", bufs=1))
         ps_c = ctx.enter_context(tc.psum_pool(name="ps_c", bufs=1))
-        ps_o = ctx.enter_context(tc.psum_pool(name="ps_o", bufs=2))
-
-        ident = const.tile([P, P], BF16, name="ident")
-        masks.make_identity(nc, ident[:])
-        ident_f = const.tile([P, P], F32, name="ident_f")
-        masks.make_identity(nc, ident_f[:])
+        ps_x = ctx.enter_context(tc.psum_pool(name="ps_x", bufs=2))
+        ctx.enter_context(tc.manual_schedule())
 
         qv = q_rot.rearrange("b h (p c) d -> p (b h) (c d)", c=NC)
         kv = k_rot.rearrange("b h (p c) d -> p (b h) (c d)", c=NC)
         vv = v.rearrange("b h (p c) d -> p (b h) (c d)", c=NC)
         wv = w_out.rearrange("(g t p) n -> p g t n", g=2, t=4)
-        q_sb, k_sb, v_sb = [], [], []
-        for i in range(NH // 2):
-            q_sb.append(keep.tile([P, 2, N], BF16, name="q%d" % i))
-            k_sb.append(keep.tile([P, 2, N], BF16, name="k%d" % i))
-            v_sb.append(keep.tile([P, 2, N], BF16, name="v%d" % i))
+        q_sb, k_sb, v_sb = {}, {}, {}
+
+        def load(dst, view, first, count, label):
+            t_in = keep.tile([P, count, N], BF16, name="%s%d" % (label, first))
+            nc.sync.dma_start(out=t_in[:], in_=view[:, first:first + count, :])
+            for h in range(count):
+                dst[first + h] = t_in[:, h, :]
+
         w_raw = [keep.tile([P, 4, D], BF16, name="wraw%d" % g) for g in range(2)]
         bias_bc = keep.tile([P, D], BF16, name="bias_bc")
-
-        def load_pair(i):
-            nc.sync.dma_start(out=q_sb[i][:], in_=qv[:, 2 * i:2 * i + 2, :])
-            nc.sync.dma_start(out=k_sb[i][:], in_=kv[:, 2 * i:2 * i + 2, :])
-            nc.sync.dma_start(out=v_sb[i][:], in_=vv[:, 2 * i:2 * i + 2, :])
-
-        load_pair(0)
-        load_pair(1)
+        load(q_sb, qv, 0, 1, "q")
+        load(k_sb, kv, 0, 1, "k")
+        load(q_sb, qv, 1, 1, "q")
+        load(k_sb, kv, 1, 1, "k")
         nc.sync.dma_start(out=w_raw[0][:], in_=wv[:, 0])
-        load_pair(2)
+        load(v_sb, vv, 0, 2, "v")
+        load(q_sb, qv, 2, 2, "q")
+        load(k_sb, kv, 2, 2, "k")
         nc.sync.dma_start(out=w_raw[1][:], in_=wv[:, 1])
-        load_pair(3)
-        nc.sync.dma_start(out=bias_bc[:], in_=b_out.partition_broadcast(P))
-        for i in range(4, NH // 2):
-            load_pair(i)
+        load(v_sb, vv, 2, 2, "v")
+        for first in range(4, NH, 2):
+            load(q_sb, qv, first, 2, "q")
+            load(k_sb, kv, first, 2, "k")
+            load(v_sb, vv, first, 2, "v")
+            if first == 4:
+                nc.sync.dma_start(out=bias_bc[:], in_=b_out.partition_broadcast(P))
+
+        ident = const.tile([P, P], BF16, name="ident")
+        masks.make_identity(nc, ident[:])
+        ident_f = const.tile([P, P], F32, name="ident_f")
+        masks.make_identity(nc, ident_f[:])
+        warm = const.tile([P, 2], F32, name="warm")
+        nc.vector.memset(warm[:], 0.0)
+        nc.scalar.activation(out=warm[:, 1:2], in_=warm[:, 0:1], func=ACT.Exp)
 
         w_grp = [keep.tile([P, D, 4], BF16, name="wgrp%d" % g, align_bytes=64) for g in range(2)]
         w_codes = keep.tile([P, 2, D], U32, name="w_codes", align_bytes=64)
         w_scales = keep.tile([P, 2, D], U8, name="w_scales", align_bytes=64)
 
-        def w_regroup(g, piece):
+        def w_regroup(eng, g, piece):
             cols = slice(piece * 256, (piece + 1) * 256)
-            nc.vector.tensor_copy(
-                out=w_grp[g][:, cols, :].rearrange("p (c i) t -> p c t i", i=4),
-                in_=w_raw[g][:, :, cols].rearrange("p t (c i) -> p c t i", i=4),
-            )
+            if eng == "gpsimd":
+                nc.gpsimd.tensor_scalar(out=w_grp[g][:, cols, :],
+                                        in0=w_raw[g][:, :, cols].rearrange("p t n -> p n t"),
+                                        scalar1=1.0, scalar2=0.0, op0=ALU.mult, op1=ALU.add)
+            else:
+                nc.scalar.copy(out=w_grp[g][:, cols, :].rearrange("p (c i) t -> p c t i", i=4),
+                               in_=w_raw[g][:, :, cols].rearrange("p t (c i) -> p c t i", i=4))
 
         def w_quant(g, half):
             cols = slice(half * 512, (half + 1) * 512)
-            nc.vector.quantize_mx(
-                out=w_codes[:, g, cols].bitcast(FP8X4),
-                scales=w_scales[:, g, cols],
-                in_=w_grp[g][:, cols, :].rearrange("p n t -> p (n t)"),
-            )
+            nc.vector.quantize_mx(out=w_codes[:, g, cols].bitcast(FP8X4), scales=w_scales[:, g, cols],
+                                  in_=w_grp[g][:, cols, :].rearrange("p n t -> p (n t)"))
 
-        qkT = {}
-        e_sb = {}
-        rsum = {}
-        a4 = {}
-        a_codes = {}
-        a_scales = {}
+        tp_ps, qkT, s_bank, e_sb, mx, nb, rs, rr = {}, {}, {}, {}, {}, {}, {}, {}
+        cg, cv, a4, ta_ps, grp, a_codes, a_scales, o_ps, o_sb = {}, {}, {}, {}, {}, {}, {}, {}, {}
 
-        def stage_t(i):
-            tp = ps_t.tile([P, 2 * N], BF16, name="tp", tag="t")
+        def tqk(h):
+            tp_ps[h] = ps_t.tile([P, 2 * N], BF16, name="tp")
             for c in range(NC):
-                nc.tensor.transpose(out=tp[:, c * P:(c + 1) * P],
-                                    in_=q_sb[i // 2][:, i % 2, c * P:(c + 1) * P], identity=ident[:])
+                nc.tensor.transpose(out=tp_ps[h][:, c * P:(c + 1) * P],
+                                    in_=q_sb[h][:, c * P:(c + 1) * P], identity=ident[:])
             for c in range(NC):
-                nc.tensor.transpose(out=tp[:, N + c * P:N + (c + 1) * P],
-                                    in_=k_sb[i // 2][:, i % 2, c * P:(c + 1) * P], identity=ident[:])
-            t_sb = qk_pool.tile([P, 2 * N], BF16, name="qkT")
-            nc.scalar.copy(out=t_sb[:], in_=tp[:])
-            qkT[i] = t_sb
+                nc.tensor.transpose(out=tp_ps[h][:, N + c * P:N + (c + 1) * P],
+                                    in_=k_sb[h][:, c * P:(c + 1) * P], identity=ident[:])
 
-        def stage_s(i):
-            t_sb = qkT[i]
-            e_t = e_pool.tile([P, NC, N], F32, name="e_t")
-            mx = st_pool.tile([P, NC], F32, name="mx")
-            nb = st_pool.tile([P, NC], F32, name="nb")
-            rs = st_pool.tile([P, NC], F32, name="rs")
-            for pair in range(2):
-                banks = []
-                for c in (2 * pair, 2 * pair + 1):
-                    s_ps = ps_s.tile([P, N], F32, name="s_ps")
-                    nc.tensor.matmul(out=s_ps[:], lhsT=t_sb[:, c * P:(c + 1) * P], rhs=t_sb[:, N:2 * N],
-                                     start=True, stop=True)
-                    nc.vector.tensor_reduce(out=mx[:, c:c + 1], in_=s_ps[:], axis=AX.X, op=ALU.max)
-                    banks.append(s_ps)
-                two = slice(2 * pair, 2 * pair + 2)
-                nc.vector.tensor_scalar(out=nb[:, two], in0=mx[:, two], scalar1=-SCALE, scalar2=None,
-                                        op0=ALU.mult)
-                for c in (2 * pair, 2 * pair + 1):
-                    nc.scalar.activation(out=e_t[:, c, :], in_=banks[c % 2][:], func=ACT.Exp,
-                                         bias=nb[:, c:c + 1], scale=SCALE, accum_out=rs[:, c:c + 1])
-            e_sb[i] = e_t
-            rsum[i] = rs
+        def evq(h):
+            qkT[h] = qk_pool.tile([P, 2 * N], BF16, name="qkT")
+            nc.scalar.copy(out=qkT[h][:], in_=tp_ps[h][:])
 
-        def stage_r(i):
-            e_t = e_sb[i]
-            rr = st_pool.tile([P, NC], F32, name="rr")
-            nc.vector.reciprocal(out=rr[:], in_=rsum[i][:])
-            for c in range(NC):
-                nc.gpsimd.tensor_scalar(out=e_t[:, c, :], in0=e_t[:, c, :], scalar1=rr[:, c:c + 1],
+        def qk_mm(s):
+            h, c = divmod(s, NC)
+            s_bank[s] = ps_s.tile([P, N], F32, name="s_ps", tag="s")
+            nc.tensor.matmul(out=s_bank[s][:], lhsT=qkT[h][:, c * P:(c + 1) * P], rhs=qkT[h][:, N:2 * N],
+                             start=True, stop=True)
+
+        def vmax(s):
+            h, c = divmod(s, NC)
+            if c == 0:
+                mx[h] = st_pool.tile([P, NC], F32, name="mx")
+            nc.vector.tensor_reduce(out=mx[h][:, c:c + 1], in_=s_bank[s][:], axis=AX.X, op=ALU.max)
+
+        def nbexp(s):
+            h, c = divmod(s, NC)
+            if c == 0:
+                nb[h] = st_pool.tile([P, NC], F32, name="nb")
+                rs[h] = st_pool.tile([P, NC], F32, name="rs")
+                e_sb[h] = e_pool.tile([P, NC, N], F32, name="e_t")
+            nc.scalar.mul(out=nb[h][:, c:c + 1], in_=mx[h][:, c:c + 1], mul=-SCALE)
+            nc.scalar.activation(out=e_sb[h][:, c, :], in_=s_bank[s][:], func=ACT.Exp,
+                                 bias=nb[h][:, c:c + 1], scale=SCALE, accum_out=rs[h][:, c:c + 1])
+
+        def rc(h):
+            rr[h] = st_pool.tile([P, NC], F32, name="rr")
+            nc.vector.reciprocal(out=rr[h][:], in_=rs[h][:])
+
+        def sc(eng, h, c):
+            if eng == "gpsimd":
+                nc.gpsimd.tensor_scalar(out=e_sb[h][:, c, :], in0=e_sb[h][:, c, :], scalar1=rr[h][:, c:c + 1],
                                         scalar2=0.0, op0=ALU.mult, op1=ALU.add)
+            elif eng == "vector":
+                nc.vector.tensor_scalar(out=e_sb[h][:, c, :], in0=e_sb[h][:, c, :], scalar1=rr[h][:, c:c + 1],
+                                        scalar2=None, op0=ALU.mult)
+            else:
+                nc.scalar.activation(out=e_sb[h][:, c, :], in_=e_sb[h][:, c, :], func=ACT.Copy,
+                                     scale=rr[h][:, c:c + 1])
 
-        def stage_g(i):
-            bg, t = i // 4, i % 4
-            e_t = e_sb[i]
-            cg = ps_c.tile([P, NC, P], F32, name="cg")
-            for j in range(NC):
-                for c in range(NC):
-                    nc.tensor.matmul(out=cg[:, j, :], lhsT=e_t[:, c, j * P:(j + 1) * P], rhs=ident_f[:],
-                                     start=(c == 0), stop=(c == NC - 1), is_transpose=True)
-            cv = st_pool.tile([P, NC], F32, name="cv")
-            nc.vector.tensor_reduce(out=cv[:], in_=cg[:], axis=AX.X, op=ALU.add)
+        def gt(h, j):
+            if j == 0 and h < NH - 2:
+                cg[h] = ps_c.tile([P, NC, P], F32, name="cg")
+            if j == 0 and h >= NH - 2:
+                cg[h] = ps_s.tile([P, NC, P], F32, name="cg_s", tag="s")
+            for c in range(NC):
+                nc.tensor.matmul(out=cg[h][:, j, :], lhsT=e_sb[h][:, c, j * P:(j + 1) * P], rhs=ident_f[:],
+                                 start=(c == 0), stop=(c == NC - 1), is_transpose=True)
+
+        def red(h):
+            cv[h] = st_pool.tile([P, NC], F32, name="cv")
+            nc.vector.tensor_reduce(out=cv[h][:], in_=cg[h][:], axis=AX.X, op=ALU.add)
+
+        def av(h):
+            bg, t = divmod(h, 4)
             if t == 0:
                 a4[bg] = a_pool.tile([P, 4, NC, DH], BF16, name="a4")
             for j in range(NC):
-                nc.vector.tensor_scalar(out=a4[bg][:, t, j, :],
-                                        in0=v_sb[i // 2][:, i % 2, j * P:(j + 1) * P],
-                                        scalar1=cv[:, j:j + 1], scalar2=None, op0=ALU.mult)
+                nc.vector.tensor_scalar(out=a4[bg][:, t, j, :], in0=v_sb[h][:, j * P:(j + 1) * P],
+                                        scalar1=cv[h][:, j:j + 1], scalar2=None, op0=ALU.mult)
 
-        def stage_a(bg):
-            grp = a_pool.tile([P, 2, 2 * P, 4], BF16, name="grp", align_bytes=64)
+        def ta(bg):
             for jj in range(2):
-                ta = ps_t.tile([P, 4, 2 * P], BF16, name="ta", tag="t")
-                for t in range(4):
-                    for jl in range(2):
-                        nc.tensor.transpose(out=ta[:, t, jl * P:(jl + 1) * P],
-                                            in_=a4[bg][:, t, 2 * jj + jl, :], identity=ident[:])
-                if jj == 0 or bg < 3:
-                    nc.scalar.copy(out=grp[:, jj, :, :], in_=ta[:].rearrange("p t x -> p x t"))
-                else:
-                    nc.vector.tensor_copy(out=grp[:, jj, :, :], in_=ta[:].rearrange("p t x -> p x t"))
+                ta_ps[bg, jj] = ps_x.tile([P, 4, 2 * P], BF16, name="ta_x", tag="x")
+            for t in range(4):
+                for j in range(NC):
+                    nc.tensor.transpose(out=ta_ps[bg, j // 2][:, t, (j % 2) * P:(j % 2 + 1) * P],
+                                        in_=a4[bg][:, t, j, :], identity=ident[:])
+
+        def eva(eng, bg, jj, half):
+            if jj == 0 and half == 0:
+                grp[bg] = a_pool.tile([P, NC, P, 4], BF16, name="grp", align_bytes=64)
+            src = ta_ps[bg, jj][:, :, half * P:(half + 1) * P].rearrange("p t x -> p x t")
+            if eng == "scalar":
+                nc.scalar.copy(out=grp[bg][:, 2 * jj + half, :, :], in_=src)
+            else:
+                nc.vector.tensor_copy(out=grp[bg][:, 2 * jj + half, :, :], in_=src)
+
+        def qa(bg):
             a_codes[bg] = keep.tile([P, N], U32, name="a_codes%d" % bg, align_bytes=64)
             a_scales[bg] = keep.tile([P, N], U8, name="a_scales%d" % bg, align_bytes=64)
             nc.vector.quantize_mx(out=a_codes[bg][:].bitcast(FP8X4), scales=a_scales[bg][:],
-                                  in_=grp[:].rearrange("p a x t -> p (a x t)"))
+                                  in_=grp[bg][:].rearrange("p j x t -> p (j x t)"))
 
         ov = out.rearrange("b (p j) n -> b j p n", j=NC)
 
-        def stage_o(b):
-            for j in range(NC):
-                o_sb = o_pool.tile([P, D], F32, name="o_sb")
-                for nh in range(2):
-                    cols = slice(nh * 512, (nh + 1) * 512)
-                    o_ps = ps_o.tile([P, 512], F32, name="o_ps")
-                    for g in range(2):
-                        nc.tensor.matmul_mx(
-                            out=o_ps[:],
-                            lhsT=a_codes[2 * b + g][:, j * P:(j + 1) * P].bitcast(FP8X4),
-                            lhsT_scale=a_scales[2 * b + g][:, j * P:(j + 1) * P],
-                            rhs=w_codes[:, g, cols].bitcast(FP8X4),
-                            rhs_scale=w_scales[:, g, cols],
-                            start=(g == 0), stop=(g == 1))
-                    nc.vector.tensor_tensor(out=o_sb[:, cols], in0=o_ps[:], in1=bias_bc[:, cols], op=ALU.add)
-                nc.sync.dma_start(out=ov[b, j], in_=o_sb[:])
+        def mx_group(b, u):
+            j, nh = divmod(u, 2)
+            cols = slice(nh * 512, (nh + 1) * 512)
+            if b == 1:
+                o_ps[b, u] = ps_s.tile([P, 512], F32, name="o_s", tag="s")
+            else:
+                o_ps[b, u] = ps_x.tile([P, 512], F32, name="o_x", tag="x")
+            for g in range(2):
+                nc.tensor.matmul_mx(out=o_ps[b, u][:],
+                                    lhsT=a_codes[2 * b + g][:, j * P:(j + 1) * P].bitcast(FP8X4),
+                                    lhsT_scale=a_scales[2 * b + g][:, j * P:(j + 1) * P],
+                                    rhs=w_codes[:, g, cols].bitcast(FP8X4), rhs_scale=w_scales[:, g, cols],
+                                    start=(g == 0), stop=(g == 1))
 
-        for step in range(NH + 3):
-            if step < NH:
-                stage_t(step)
-            if 1 <= step <= NH:
-                stage_s(step - 1)
-            if 2 <= step <= NH + 1:
-                stage_r(step - 2)
-            if 2 <= step <= 5:
-                g = (step - 2) // 2
-                for piece in range(2):
-                    w_regroup(g, 2 * ((step - 2) % 2) + piece)
-                w_quant(g, (step - 2) % 2)
-            if step >= 3:
-                i = step - 3
-                stage_g(i)
-                if i % 4 == 3:
-                    stage_a(i // 4)
-                if i % 8 == 7:
-                    stage_o(i // 8)
+        def out_group(b, u):
+            j, nh = divmod(u, 2)
+            cols = slice(nh * 512, (nh + 1) * 512)
+            if nh == 0:
+                o_sb[b, j] = o_pool.tile([P, D], F32, name="o_sb")
+            nc.vector.tensor_tensor(out=o_sb[b, j][:, cols], in0=o_ps[b, u][:], in1=bias_bc[:, cols], op=ALU.add)
+            if nh == 1:
+                nc.sync.dma_start(out=ov[b, j], in_=o_sb[b, j][:])
+
+        for h in range(2):
+            tqk(h)
+            evq(h)
+        qk_mm(0)
+        for piece in range(4):
+            w_regroup("gpsimd", 0, piece)
+        for s in range((NH + 4) * NC):
+            i, k = divmod(s, NC)
+            bg, since = divmod(i - 7, 4)
+            if s + 1 < NS:
+                qk_mm(s + 1)
+            if k == 3 and i + 2 < NH:
+                tqk(i + 2)
+            if 0 <= i - 3 < NH:
+                if k == 0:
+                    gt(i - 3, 0)
+                if k == 1:
+                    gt(i - 3, 1)
+                    gt(i - 3, 2)
+                if k == 2:
+                    gt(i - 3, 3)
+            if k == 2 and since == 0 and 0 <= bg < 4:
+                ta(bg)
+            if s < NS:
+                vmax(s)
+            if k == 1 and 0 <= i - 1 < NH:
+                rc(i - 1)
+                if i - 1 == NH - 1:
+                    sc("vector", i - 1, 1)
+                    sc("vector", i - 1, 3)
+            if k == 3 and 0 <= i - 3 < NH:
+                red(i - 3)
+            if k == 0 and 0 <= i - 4 < NH:
+                av(i - 4)
+            if k == 0 and since == 2 and 0 <= bg < 3:
+                qa(bg)
+            if k == 2 and 4 <= i < 8:
+                w_quant((i - 4) // 2, (i - 4) % 2)
+            if s < NS:
+                nbexp(s)
+            if k == 0 and 1 <= i + 1 < NH and i >= 1:
+                evq(i + 1)
+            if k == 1 and i - 1 == NH - 1:
+                sc("scalar", i - 1, 2)
+            piece = 4 * since + k - 3
+            if 0 <= bg < 3 and 0 <= piece < 4:
+                eva("scalar", bg, piece // 2, piece % 2)
+            if k == 3 and 1 <= i <= 4:
+                w_regroup("scalar", 1, i - 1)
+            h, c = divmod(s - 5, NC)
+            if 0 <= h < NH - 1 or (h == NH - 1 and c == 0):
+                sc("gpsimd", h, c)
+            if bg == 1 and since == 2 and k == 2:
+                for u in range(8):
+                    mx_group(0, u)
+                    out_group(0, u)
+            if bg == 3 and since == 0 and k == 3:
+                eva("scalar", bg, 0, 0)
+                eva("vector", bg, 0, 1)
+                eva("scalar", bg, 1, 0)
+                eva("vector", bg, 1, 1)
+                qa(bg)
+                for u in range(8):
+                    mx_group(1, u)
+                    out_group(1, u)

@@ -124,13 +124,17 @@ def tile_attn_pb_kernel(tc, q_rot, k_rot, v, w_out, b_out, out):
                 mx[h] = st_pool.tile([P, NC], F32, name="mx")
             nc.vector.tensor_reduce(out=mx[h][:, c:c + 1], in_=s_bank[s][:], axis=AX.X, op=ALU.max)
 
-        def nbexp(s):
+        def nbias(s):
             h, c = divmod(s, NC)
             if c == 0:
                 nb[h] = st_pool.tile([P, NC], F32, name="nb")
+            nc.scalar.mul(out=nb[h][:, c:c + 1], in_=mx[h][:, c:c + 1], mul=-SCALE)
+
+        def expo(s):
+            h, c = divmod(s, NC)
+            if c == 0:
                 rs[h] = st_pool.tile([P, NC], F32, name="rs")
                 e_sb[h] = e_pool.tile([P, NC, N], F32, name="e_t")
-            nc.scalar.mul(out=nb[h][:, c:c + 1], in_=mx[h][:, c:c + 1], mul=-SCALE)
             nc.scalar.activation(out=e_sb[h][:, c, :], in_=s_bank[s][:], func=ACT.Exp,
                                  bias=nb[h][:, c:c + 1], scale=SCALE, accum_out=rs[h][:, c:c + 1])
 
@@ -218,18 +222,14 @@ def tile_attn_pb_kernel(tc, q_rot, k_rot, v, w_out, b_out, out):
             if nh == 1:
                 nc.sync.dma_start(out=ov[b, j], in_=o_sb[b, j][:])
 
-        for h in range(2):
-            tqk(h)
-            evq(h)
-        qk_mm(0)
         for piece in range(4):
             w_regroup("gpsimd", 0, piece)
-        for s in range((NH + 4) * NC):
+        for s in range(-5, (NH + 4) * NC):
             i, k = divmod(s, NC)
             bg, since = divmod(i - 7, 4)
-            if s + 1 < NS:
+            if 0 <= s + 1 < NS:
                 qk_mm(s + 1)
-            if k == 3 and i + 2 < NH:
+            if k == 3 and 0 <= i + 2 < NH:
                 tqk(i + 2)
             if 0 <= i - 3 < NH:
                 if k == 0:
@@ -241,9 +241,9 @@ def tile_attn_pb_kernel(tc, q_rot, k_rot, v, w_out, b_out, out):
                     gt(i - 3, 3)
             if k == 2 and since == 0 and 0 <= bg < 4:
                 ta(bg)
-            if s < NS:
+            if 0 <= s < NS:
                 vmax(s)
-            if k == 1 and 0 <= i - 1 < NH:
+            if k == 2 and 0 <= i - 1 < NH:
                 rc(i - 1)
                 if i - 1 == NH - 1:
                     sc("vector", i - 1, 1)
@@ -254,22 +254,24 @@ def tile_attn_pb_kernel(tc, q_rot, k_rot, v, w_out, b_out, out):
                 av(i - 4)
             if k == 0 and since == 2 and 0 <= bg < 3:
                 qa(bg)
-            if k == 2 and 4 <= i < 8:
-                w_quant((i - 4) // 2, (i - 4) % 2)
-            if s < NS:
-                nbexp(s)
-            if k == 0 and 1 <= i + 1 < NH and i >= 1:
+            if k == 2 and 6 <= i < 10:
+                w_quant((i - 6) // 2, (i - 6) % 2)
+            if 0 <= s < NS:
+                nbias(s)
+            if 0 <= s - 1 < NS:
+                expo(s - 1)
+            if k == 0 and 0 <= i + 1 < NH:
                 evq(i + 1)
-            if k == 1 and i - 1 == NH - 1:
+            if k == 2 and i - 1 == NH - 1:
                 sc("scalar", i - 1, 2)
             piece = 4 * since + k - 3
             if 0 <= bg < 3 and 0 <= piece < 4:
                 eva("scalar", bg, piece // 2, piece % 2)
-            if k == 3 and 1 <= i <= 4:
-                w_regroup("scalar", 1, i - 1)
-            h, c = divmod(s - 5, NC)
+            h, c = divmod(s - 6, NC)
             if 0 <= h < NH - 1 or (h == NH - 1 and c == 0):
                 sc("gpsimd", h, c)
+            if 0 <= h < 4 and c == 3:
+                w_regroup("gpsimd", 1, h)
             if bg == 1 and since == 2 and k == 2:
                 for u in range(8):
                     mx_group(0, u)

@@ -197,6 +197,14 @@ def tile_attn_pb_kernel(tc, q_rot, k_rot, v, w_out, b_out, out):
             nc.vector.quantize_mx(out=a_codes[bg][:].bitcast(FP8X4), scales=a_scales[bg][:],
                                   in_=grp[bg][:].rearrange("p j x t -> p (j x t)"))
 
+        def qa_half(bg, jj):
+            if jj == 0:
+                a_codes[bg] = keep.tile([P, N], U32, name="a_codes%d" % bg, align_bytes=64)
+                a_scales[bg] = keep.tile([P, N], U8, name="a_scales%d" % bg, align_bytes=64)
+            cols = slice(jj * 2 * P, (jj + 1) * 2 * P)
+            nc.vector.quantize_mx(out=a_codes[bg][:, cols].bitcast(FP8X4), scales=a_scales[bg][:, cols],
+                                  in_=grp[bg][:, 2 * jj:2 * jj + 2, :, :].rearrange("p j x t -> p (j x t)"))
+
         ov = out.rearrange("b (p j) n -> b j p n", j=NC)
 
         def mx_group(b, u):
@@ -246,12 +254,14 @@ def tile_attn_pb_kernel(tc, q_rot, k_rot, v, w_out, b_out, out):
             if k == 2 and 0 <= i - 1 < NH:
                 rc(i - 1)
                 if i - 1 == NH - 1:
-                    sc("vector", i - 1, 1)
-                    sc("vector", i - 1, 3)
+                    sc("vector", i - 1, 0)
+                    sc("vector", i - 1, 2)
             if k == 3 and 0 <= i - 3 < NH:
                 red(i - 3)
             if k == 0 and 0 <= i - 4 < NH:
                 av(i - 4)
+            if k == 0 and 0 <= i - 2 < NH - 1:
+                sc("vector", i - 2, 3)
             if k == 0 and since == 2 and 0 <= bg < 3:
                 qa(bg)
             if k == 2 and 6 <= i < 10:
@@ -263,12 +273,13 @@ def tile_attn_pb_kernel(tc, q_rot, k_rot, v, w_out, b_out, out):
             if k == 0 and 0 <= i + 1 < NH:
                 evq(i + 1)
             if k == 2 and i - 1 == NH - 1:
-                sc("scalar", i - 1, 2)
+                sc("scalar", i - 1, 1)
+                sc("scalar", i - 1, 3)
             piece = 4 * since + k - 3
             if 0 <= bg < 3 and 0 <= piece < 4:
                 eva("scalar", bg, piece // 2, piece % 2)
             h, c = divmod(s - 6, NC)
-            if 0 <= h < NH - 1 or (h == NH - 1 and c == 0):
+            if 0 <= h < NH - 1 and c < 3:
                 sc("gpsimd", h, c)
             if 0 <= h < 4 and c == 3:
                 w_regroup("gpsimd", 1, h)
@@ -277,11 +288,10 @@ def tile_attn_pb_kernel(tc, q_rot, k_rot, v, w_out, b_out, out):
                     mx_group(0, u)
                     out_group(0, u)
             if bg == 3 and since == 0 and k == 3:
-                eva("scalar", bg, 0, 0)
-                eva("vector", bg, 0, 1)
-                eva("scalar", bg, 1, 0)
-                eva("vector", bg, 1, 1)
-                qa(bg)
+                for jj in range(2):
+                    eva("scalar", bg, jj, 0)
+                    eva("vector", bg, jj, 1)
+                    qa_half(bg, jj)
                 for u in range(8):
                     mx_group(1, u)
                     out_group(1, u)

@@ -264,8 +264,10 @@ def tile_attn_pb_kernel(tc, q_rot, k_rot, v, w_out, b_out, out):
                 sc("vector", i - 2, 3)
             if k == 0 and since == 2 and 0 <= bg < 3:
                 qa(bg)
-            if k == 2 and 6 <= i < 10:
-                w_quant((i - 6) // 2, (i - 6) % 2)
+            if k == 2 and 5 <= i < 7:
+                w_quant(0, i - 5)
+            if k == 2 and 11 <= i < 13:
+                w_quant(1, i - 11)
             if 0 <= s < NS:
                 nbias(s)
             if 0 <= s - 1 < NS:
@@ -281,8 +283,8 @@ def tile_attn_pb_kernel(tc, q_rot, k_rot, v, w_out, b_out, out):
             h, c = divmod(s - 6, NC)
             if 0 <= h < NH - 1 and c < 3:
                 sc("gpsimd", h, c)
-            if 0 <= h < 4 and c == 3:
-                w_regroup("gpsimd", 1, h)
+            if 5 <= h < 9 and c == 3:
+                w_regroup("gpsimd", 1, h - 5)
             if bg == 1 and since == 2 and k == 2:
                 for u in range(8):
                     mx_group(0, u)

@@ -14,12 +14,32 @@ ALU = mybir.AluOpType
 AX = mybir.AxisListType
 
 P = 128
-B, H, N, DH, D = 2, 8, 512, 128, 1024
-NH = B * H
-NC = N // P
-NS = NH * NC
-SCALE = math.sqrt(DH)
-FLOPS = 2 * NH * N * N * DH + 2 * NH * N * N + 2 * B * N * H * DH * D
+BATCHES, HEADS_PER_BATCH, TOKENS, D_OUT = 2, 8, 512, 1024
+HEADS = BATCHES * HEADS_PER_BATCH
+CHUNKS = TOKENS // P
+ALL_CHUNKS = HEADS * CHUNKS
+PACK = 4
+GROUPS = HEADS // PACK
+PARTS = GROUPS // BATCHES
+N_MX = 512
+SCALE = math.sqrt(P)
+FLOPS = 2 * HEADS * TOKENS * TOKENS * (P + 1) + 2 * BATCHES * TOKENS * HEADS_PER_BATCH * P * D_OUT
+
+TRANSPOSE_QK = -5
+COPY_QK = -4
+RECIPROCAL = 6
+SCALE_GPSIMD = 6
+SCALE_VECTOR = 8
+GATE = (12, 13, 13, 14)
+REDUCE = 15
+WEIGH = 16
+GROUP_READY = CHUNKS * (PACK - 1) + WEIGH
+TRANSPOSE_A = 2
+COPY_A = 3
+QUANTISE_A = 8
+PROJECT = 10
+W_LATE_HEAD = 5
+W_QUANTISE = ((22, 26), (46, 50))
 
 
 def tile_attn_pb_kernel(tc, q_rot, k_rot, v, w_out, b_out, out):
@@ -31,43 +51,41 @@ def tile_attn_pb_kernel(tc, q_rot, k_rot, v, w_out, b_out, out):
         e_pool = ctx.enter_context(tc.tile_pool(name="e", bufs=5))
         st_pool = ctx.enter_context(tc.tile_pool(name="stat", bufs=6))
         a_pool = ctx.enter_context(tc.tile_pool(name="a", bufs=2))
-        o_pool = ctx.enter_context(tc.tile_pool(name="o", bufs=4))
+        o_pool = ctx.enter_context(tc.tile_pool(name="o", bufs=6))
         ps_s = ctx.enter_context(tc.psum_pool(name="ps_s", bufs=4))
         ps_t = ctx.enter_context(tc.psum_pool(name="ps_t", bufs=1))
         ps_c = ctx.enter_context(tc.psum_pool(name="ps_c", bufs=1))
         ps_x = ctx.enter_context(tc.psum_pool(name="ps_x", bufs=2))
         ctx.enter_context(tc.manual_schedule())
 
-        qv = q_rot.rearrange("b h (p c) d -> p (b h) (c d)", c=NC)
-        kv = k_rot.rearrange("b h (p c) d -> p (b h) (c d)", c=NC)
-        vv = v.rearrange("b h (p c) d -> p (b h) (c d)", c=NC)
-        wv = w_out.rearrange("(g t p) n -> p g t n", g=2, t=4)
+        q_view = q_rot.rearrange("b h (p c) d -> p (b h) (c d)", c=CHUNKS)
+        k_view = k_rot.rearrange("b h (p c) d -> p (b h) (c d)", c=CHUNKS)
+        v_view = v.rearrange("b h (p c) d -> p (b h) (c d)", c=CHUNKS)
+        w_view = w_out.rearrange("(r t p) n -> p r t n", r=PARTS, t=PACK)
         q_sb, k_sb, v_sb = {}, {}, {}
 
         def load(dst, view, first, count, label):
-            t_in = keep.tile([P, count, N], BF16, name="%s%d" % (label, first))
+            t_in = keep.tile([P, count, TOKENS], BF16, name="%s%d" % (label, first))
             nc.sync.dma_start(out=t_in[:], in_=view[:, first:first + count, :])
             for h in range(count):
                 dst[first + h] = t_in[:, h, :]
 
-        w_raw = [keep.tile([P, 4, D], BF16, name="wraw%d" % g) for g in range(2)]
-        bias_bc = keep.tile([P, D], BF16, name="bias_bc")
-        load(q_sb, qv, 0, 1, "q")
-        load(k_sb, kv, 0, 1, "k")
-        load(q_sb, qv, 1, 1, "q")
-        load(k_sb, kv, 1, 1, "k")
-        nc.sync.dma_start(out=w_raw[0][:], in_=wv[:, 0])
-        load(v_sb, vv, 0, 2, "v")
-        load(q_sb, qv, 2, 2, "q")
-        load(k_sb, kv, 2, 2, "k")
-        nc.sync.dma_start(out=w_raw[1][:], in_=wv[:, 1])
-        load(v_sb, vv, 2, 2, "v")
-        for first in range(4, NH, 2):
-            load(q_sb, qv, first, 2, "q")
-            load(k_sb, kv, first, 2, "k")
-            load(v_sb, vv, first, 2, "v")
-            if first == 4:
-                nc.sync.dma_start(out=bias_bc[:], in_=b_out.partition_broadcast(P))
+        w_raw = [keep.tile([P, PACK, D_OUT], BF16, name="wraw%d" % r) for r in range(PARTS)]
+        bias_bc = keep.tile([P, D_OUT], BF16, name="bias_bc")
+        for h in range(2):
+            load(q_sb, q_view, h, 1, "q")
+            load(k_sb, k_view, h, 1, "k")
+        nc.sync.dma_start(out=w_raw[0][:], in_=w_view[:, 0])
+        load(v_sb, v_view, 0, 2, "v")
+        load(q_sb, q_view, 2, 2, "q")
+        load(k_sb, k_view, 2, 2, "k")
+        nc.sync.dma_start(out=w_raw[1][:], in_=w_view[:, 1])
+        load(v_sb, v_view, 2, 2, "v")
+        nc.sync.dma_start(out=bias_bc[:], in_=b_out.partition_broadcast(P))
+        for first in range(4, HEADS, 2):
+            load(q_sb, q_view, first, 2, "q")
+            load(k_sb, k_view, first, 2, "k")
+            load(v_sb, v_view, first, 2, "v")
 
         ident = const.tile([P, P], BF16, name="ident")
         masks.make_identity(nc, ident[:])
@@ -77,223 +95,206 @@ def tile_attn_pb_kernel(tc, q_rot, k_rot, v, w_out, b_out, out):
         nc.vector.memset(warm[:], 0.0)
         nc.scalar.activation(out=warm[:, 1:2], in_=warm[:, 0:1], func=ACT.Exp)
 
-        w_grp = [keep.tile([P, D, 4], BF16, name="wgrp%d" % g, align_bytes=64) for g in range(2)]
-        w_codes = keep.tile([P, 2, D], U32, name="w_codes", align_bytes=64)
-        w_scales = keep.tile([P, 2, D], U8, name="w_scales", align_bytes=64)
+        w_grouped = [keep.tile([P, D_OUT, PACK], BF16, name="wgrp%d" % r, align_bytes=64) for r in range(PARTS)]
+        w_codes = keep.tile([P, PARTS, D_OUT], U32, name="w_codes", align_bytes=64)
+        w_scales = keep.tile([P, PARTS, D_OUT], U8, name="w_scales", align_bytes=64)
 
-        def w_regroup(eng, g, piece):
-            cols = slice(piece * 256, (piece + 1) * 256)
-            if eng == "gpsimd":
-                nc.gpsimd.tensor_scalar(out=w_grp[g][:, cols, :],
-                                        in0=w_raw[g][:, :, cols].rearrange("p t n -> p n t"),
-                                        scalar1=1.0, scalar2=0.0, op0=ALU.mult, op1=ALU.add)
-            else:
-                nc.scalar.copy(out=w_grp[g][:, cols, :].rearrange("p (c i) t -> p c t i", i=4),
-                               in_=w_raw[g][:, :, cols].rearrange("p t (c i) -> p c t i", i=4))
+        def regroup_w(r, quarter):
+            cols = slice(quarter * D_OUT // 4, (quarter + 1) * D_OUT // 4)
+            nc.gpsimd.tensor_scalar(out=w_grouped[r][:, cols, :],
+                                    in0=w_raw[r][:, :, cols].rearrange("p t n -> p n t"),
+                                    scalar1=1.0, scalar2=0.0, op0=ALU.mult, op1=ALU.add)
 
-        def w_quant(g, half):
-            cols = slice(half * 512, (half + 1) * 512)
-            nc.vector.quantize_mx(out=w_codes[:, g, cols].bitcast(FP8X4), scales=w_scales[:, g, cols],
-                                  in_=w_grp[g][:, cols, :].rearrange("p n t -> p (n t)"))
+        def quantise_w(r, half):
+            cols = slice(half * N_MX, (half + 1) * N_MX)
+            nc.vector.quantize_mx(out=w_codes[:, r, cols].bitcast(FP8X4), scales=w_scales[:, r, cols],
+                                  in_=w_grouped[r][:, cols, :].rearrange("p n t -> p (n t)"))
 
-        tp_ps, qkT, s_bank, e_sb, mx, nb, rs, rr = {}, {}, {}, {}, {}, {}, {}, {}
-        cg, cv, a4, ta_ps, grp, a_codes, a_scales, o_ps, o_sb = {}, {}, {}, {}, {}, {}, {}, {}, {}
+        qk_ps, qk_t, score, expo, gate_ps = {}, {}, {}, {}, {}
+        row_max, bias, row_sum, inv_sum, gate = {}, {}, {}, {}, {}
 
-        def tqk(h):
-            tp_ps[h] = ps_t.tile([P, 2 * N], BF16, name="tp")
-            for c in range(NC):
-                nc.tensor.transpose(out=tp_ps[h][:, c * P:(c + 1) * P],
-                                    in_=q_sb[h][:, c * P:(c + 1) * P], identity=ident[:])
-            for c in range(NC):
-                nc.tensor.transpose(out=tp_ps[h][:, N + c * P:N + (c + 1) * P],
-                                    in_=k_sb[h][:, c * P:(c + 1) * P], identity=ident[:])
+        def transpose_qk(h):
+            qk_ps[h] = ps_t.tile([P, 2 * TOKENS], BF16, name="tp")
+            for half, src in enumerate((q_sb[h], k_sb[h])):
+                for c in range(CHUNKS):
+                    nc.tensor.transpose(out=qk_ps[h][:, half * TOKENS + c * P:half * TOKENS + (c + 1) * P],
+                                        in_=src[:, c * P:(c + 1) * P], identity=ident[:])
 
-        def evq(h):
-            qkT[h] = qk_pool.tile([P, 2 * N], BF16, name="qkT")
-            nc.scalar.copy(out=qkT[h][:], in_=tp_ps[h][:])
+        def copy_qk(h):
+            qk_t[h] = qk_pool.tile([P, 2 * TOKENS], BF16, name="qkT")
+            nc.scalar.copy(out=qk_t[h][:], in_=qk_ps[h][:])
 
-        def qk_mm(s):
-            h, c = divmod(s, NC)
-            s_bank[s] = ps_s.tile([P, N], F32, name="s_ps", tag="s")
-            nc.tensor.matmul(out=s_bank[s][:], lhsT=qkT[h][:, c * P:(c + 1) * P], rhs=qkT[h][:, N:2 * N],
+        def scores(s):
+            h, c = divmod(s, CHUNKS)
+            score[s] = ps_s.tile([P, TOKENS], F32, name="s_ps", tag="s")
+            nc.tensor.matmul(out=score[s][:], lhsT=qk_t[h][:, c * P:(c + 1) * P], rhs=qk_t[h][:, TOKENS:],
                              start=True, stop=True)
 
-        def vmax(s):
-            h, c = divmod(s, NC)
+        def maximum(s):
+            h, c = divmod(s, CHUNKS)
             if c == 0:
-                mx[h] = st_pool.tile([P, NC], F32, name="mx")
-            nc.vector.tensor_reduce(out=mx[h][:, c:c + 1], in_=s_bank[s][:], axis=AX.X, op=ALU.max)
+                row_max[h] = st_pool.tile([P, CHUNKS], F32, name="mx")
+            nc.vector.tensor_reduce(out=row_max[h][:, c:c + 1], in_=score[s][:], axis=AX.X, op=ALU.max)
 
-        def nbias(s):
-            h, c = divmod(s, NC)
+        def exp_bias(s):
+            h, c = divmod(s, CHUNKS)
             if c == 0:
-                nb[h] = st_pool.tile([P, NC], F32, name="nb")
-            nc.scalar.mul(out=nb[h][:, c:c + 1], in_=mx[h][:, c:c + 1], mul=-SCALE)
+                bias[h] = st_pool.tile([P, CHUNKS], F32, name="nb")
+            nc.scalar.mul(out=bias[h][:, c:c + 1], in_=row_max[h][:, c:c + 1], mul=-SCALE)
 
-        def expo(s):
-            h, c = divmod(s, NC)
+        def exponentials(s):
+            h, c = divmod(s, CHUNKS)
             if c == 0:
-                rs[h] = st_pool.tile([P, NC], F32, name="rs")
-                e_sb[h] = e_pool.tile([P, NC, N], F32, name="e_t")
-            nc.scalar.activation(out=e_sb[h][:, c, :], in_=s_bank[s][:], func=ACT.Exp,
-                                 bias=nb[h][:, c:c + 1], scale=SCALE, accum_out=rs[h][:, c:c + 1])
+                row_sum[h] = st_pool.tile([P, CHUNKS], F32, name="rs")
+                expo[h] = e_pool.tile([P, CHUNKS, TOKENS], F32, name="e_t")
+            nc.scalar.activation(out=expo[h][:, c, :], in_=score[s][:], func=ACT.Exp,
+                                 bias=bias[h][:, c:c + 1], scale=SCALE, accum_out=row_sum[h][:, c:c + 1])
 
-        def rc(h):
-            rr[h] = st_pool.tile([P, NC], F32, name="rr")
-            nc.vector.reciprocal(out=rr[h][:], in_=rs[h][:])
+        def reciprocal(h):
+            inv_sum[h] = st_pool.tile([P, CHUNKS], F32, name="rr")
+            nc.vector.reciprocal(out=inv_sum[h][:], in_=row_sum[h][:])
 
-        def sc(eng, h, c):
-            if eng == "gpsimd":
-                nc.gpsimd.tensor_scalar(out=e_sb[h][:, c, :], in0=e_sb[h][:, c, :], scalar1=rr[h][:, c:c + 1],
-                                        scalar2=0.0, op0=ALU.mult, op1=ALU.add)
-            elif eng == "vector":
-                nc.vector.tensor_scalar(out=e_sb[h][:, c, :], in0=e_sb[h][:, c, :], scalar1=rr[h][:, c:c + 1],
-                                        scalar2=None, op0=ALU.mult)
-            else:
-                nc.scalar.activation(out=e_sb[h][:, c, :], in_=e_sb[h][:, c, :], func=ACT.Copy,
-                                     scale=rr[h][:, c:c + 1])
+        def scale_gpsimd(h, c):
+            nc.gpsimd.tensor_scalar(out=expo[h][:, c, :], in0=expo[h][:, c, :], scalar1=inv_sum[h][:, c:c + 1],
+                                    scalar2=0.0, op0=ALU.mult, op1=ALU.add)
 
-        def gt(h, j):
-            if j == 0 and h < NH - 2:
-                cg[h] = ps_c.tile([P, NC, P], F32, name="cg")
-            if j == 0 and h >= NH - 2:
-                cg[h] = ps_s.tile([P, NC, P], F32, name="cg_s", tag="s")
-            for c in range(NC):
-                nc.tensor.matmul(out=cg[h][:, j, :], lhsT=e_sb[h][:, c, j * P:(j + 1) * P], rhs=ident_f[:],
-                                 start=(c == 0), stop=(c == NC - 1), is_transpose=True)
+        def scale_vector(h, c):
+            nc.vector.tensor_scalar(out=expo[h][:, c, :], in0=expo[h][:, c, :], scalar1=inv_sum[h][:, c:c + 1],
+                                    scalar2=None, op0=ALU.mult)
 
-        def red(h):
-            cv[h] = st_pool.tile([P, NC], F32, name="cv")
-            nc.vector.tensor_reduce(out=cv[h][:], in_=cg[h][:], axis=AX.X, op=ALU.add)
+        def scale_scalar(h, c):
+            nc.scalar.activation(out=expo[h][:, c, :], in_=expo[h][:, c, :], func=ACT.Copy,
+                                 scale=inv_sum[h][:, c:c + 1])
 
-        def av(h):
-            bg, t = divmod(h, 4)
+        def gate_sum(h, j):
+            if j == 0 and h < HEADS - 2:
+                gate_ps[h] = ps_c.tile([P, CHUNKS, P], F32, name="cg")
+            if j == 0 and h >= HEADS - 2:
+                gate_ps[h] = ps_s.tile([P, CHUNKS, P], F32, name="cg_s", tag="s")
+            for c in range(CHUNKS):
+                nc.tensor.matmul(out=gate_ps[h][:, j, :], lhsT=expo[h][:, c, j * P:(j + 1) * P], rhs=ident_f[:],
+                                 start=(c == 0), stop=(c == CHUNKS - 1), is_transpose=True)
+
+        def reduce_gate(h):
+            gate[h] = st_pool.tile([P, CHUNKS], F32, name="cv")
+            nc.vector.tensor_reduce(out=gate[h][:], in_=gate_ps[h][:], axis=AX.X, op=ALU.add)
+
+        weighed, a_ps, a_grouped, a_codes, a_scales = {}, {}, {}, {}, {}
+
+        def weigh(h):
+            g, t = divmod(h, PACK)
             if t == 0:
-                a4[bg] = a_pool.tile([P, 4, NC, DH], BF16, name="a4")
-            for j in range(NC):
-                nc.vector.tensor_scalar(out=a4[bg][:, t, j, :], in0=v_sb[h][:, j * P:(j + 1) * P],
-                                        scalar1=cv[h][:, j:j + 1], scalar2=None, op0=ALU.mult)
+                weighed[g] = a_pool.tile([P, PACK, CHUNKS, P], BF16, name="a4")
+            for j in range(CHUNKS):
+                nc.vector.tensor_scalar(out=weighed[g][:, t, j, :], in0=v_sb[h][:, j * P:(j + 1) * P],
+                                        scalar1=gate[h][:, j:j + 1], scalar2=None, op0=ALU.mult)
 
-        def ta(bg):
-            for jj in range(2):
-                ta_ps[bg, jj] = ps_x.tile([P, 4, 2 * P], BF16, name="ta_x", tag="x")
-            for t in range(4):
-                for j in range(NC):
-                    nc.tensor.transpose(out=ta_ps[bg, j // 2][:, t, (j % 2) * P:(j % 2 + 1) * P],
-                                        in_=a4[bg][:, t, j, :], identity=ident[:])
+        def transpose_a(g):
+            for pair in range(CHUNKS // 2):
+                a_ps[g, pair] = ps_x.tile([P, PACK, 2 * P], BF16, name="ta_x", tag="x")
+            for t in range(PACK):
+                for j in range(CHUNKS):
+                    nc.tensor.transpose(out=a_ps[g, j // 2][:, t, (j % 2) * P:(j % 2 + 1) * P],
+                                        in_=weighed[g][:, t, j, :], identity=ident[:])
 
-        def eva(eng, bg, jj, half):
-            if jj == 0 and half == 0:
-                grp[bg] = a_pool.tile([P, NC, P, 4], BF16, name="grp", align_bytes=64)
-            src = ta_ps[bg, jj][:, :, half * P:(half + 1) * P].rearrange("p t x -> p x t")
-            if eng == "scalar":
-                nc.scalar.copy(out=grp[bg][:, 2 * jj + half, :, :], in_=src)
-            else:
-                nc.vector.tensor_copy(out=grp[bg][:, 2 * jj + half, :, :], in_=src)
+        def copy_a(copy, g, j):
+            if j == 0:
+                a_grouped[g] = a_pool.tile([P, CHUNKS, P, PACK], BF16, name="grp", align_bytes=64)
+            copy(out=a_grouped[g][:, j, :, :],
+                 in_=a_ps[g, j // 2][:, :, (j % 2) * P:(j % 2 + 1) * P].rearrange("p t x -> p x t"))
 
-        def qa(bg):
-            a_codes[bg] = keep.tile([P, N], U32, name="a_codes%d" % bg, align_bytes=64)
-            a_scales[bg] = keep.tile([P, N], U8, name="a_scales%d" % bg, align_bytes=64)
-            nc.vector.quantize_mx(out=a_codes[bg][:].bitcast(FP8X4), scales=a_scales[bg][:],
-                                  in_=grp[bg][:].rearrange("p j x t -> p (j x t)"))
+        def quantise_a(g, pair):
+            if pair == 0:
+                a_codes[g] = keep.tile([P, TOKENS], U32, name="a_codes%d" % g, align_bytes=64)
+                a_scales[g] = keep.tile([P, TOKENS], U8, name="a_scales%d" % g, align_bytes=64)
+            cols = slice(pair * 2 * P, (pair + 1) * 2 * P)
+            nc.vector.quantize_mx(out=a_codes[g][:, cols].bitcast(FP8X4), scales=a_scales[g][:, cols],
+                                  in_=a_grouped[g][:, 2 * pair:2 * pair + 2].rearrange("p j x t -> p (j x t)"))
 
-        def qa_half(bg, jj):
-            if jj == 0:
-                a_codes[bg] = keep.tile([P, N], U32, name="a_codes%d" % bg, align_bytes=64)
-                a_scales[bg] = keep.tile([P, N], U8, name="a_scales%d" % bg, align_bytes=64)
-            cols = slice(jj * 2 * P, (jj + 1) * 2 * P)
-            nc.vector.quantize_mx(out=a_codes[bg][:, cols].bitcast(FP8X4), scales=a_scales[bg][:, cols],
-                                  in_=grp[bg][:, 2 * jj:2 * jj + 2, :, :].rearrange("p j x t -> p (j x t)"))
+        out_view = out.rearrange("b (p j) n -> b j p n", j=CHUNKS)
 
-        ov = out.rearrange("b (p j) n -> b j p n", j=NC)
+        def project(b):
+            for j in range(CHUNKS):
+                for half in range(D_OUT // N_MX):
+                    cols = slice(half * N_MX, (half + 1) * N_MX)
+                    if b == BATCHES - 1:
+                        acc = ps_s.tile([P, N_MX], F32, name="o_s", tag="s")
+                    else:
+                        acc = ps_x.tile([P, N_MX], F32, name="o_x", tag="x")
+                    for r in range(PARTS):
+                        g = PARTS * b + r
+                        nc.tensor.matmul_mx(out=acc[:],
+                                            lhsT=a_codes[g][:, j * P:(j + 1) * P].bitcast(FP8X4),
+                                            lhsT_scale=a_scales[g][:, j * P:(j + 1) * P],
+                                            rhs=w_codes[:, r, cols].bitcast(FP8X4), rhs_scale=w_scales[:, r, cols],
+                                            start=(r == 0), stop=(r == PARTS - 1))
+                    o_sb = o_pool.tile([P, N_MX], F32, name="o_sb")
+                    nc.vector.tensor_tensor(out=o_sb[:], in0=acc[:], in1=bias_bc[:, cols], op=ALU.add)
+                    nc.sync.dma_start(out=out_view[b, j][:, cols], in_=o_sb[:])
 
-        def mx_group(b, u):
-            j, nh = divmod(u, 2)
-            cols = slice(nh * 512, (nh + 1) * 512)
-            if b == 1:
-                o_ps[b, u] = ps_s.tile([P, 512], F32, name="o_s", tag="s")
-            else:
-                o_ps[b, u] = ps_x.tile([P, 512], F32, name="o_x", tag="x")
-            for g in range(2):
-                nc.tensor.matmul_mx(out=o_ps[b, u][:],
-                                    lhsT=a_codes[2 * b + g][:, j * P:(j + 1) * P].bitcast(FP8X4),
-                                    lhsT_scale=a_scales[2 * b + g][:, j * P:(j + 1) * P],
-                                    rhs=w_codes[:, g, cols].bitcast(FP8X4), rhs_scale=w_scales[:, g, cols],
-                                    start=(g == 0), stop=(g == 1))
+        def head_in(s, stage):
+            h, rest = divmod(s - stage, CHUNKS)
+            return h if rest == 0 and 0 <= h < HEADS else -1
 
-        def out_group(b, u):
-            j, nh = divmod(u, 2)
-            cols = slice(nh * 512, (nh + 1) * 512)
-            if nh == 0:
-                o_sb[b, j] = o_pool.tile([P, D], F32, name="o_sb")
-            nc.vector.tensor_tensor(out=o_sb[b, j][:, cols], in0=o_ps[b, u][:], in1=bias_bc[:, cols], op=ALU.add)
-            if nh == 1:
-                nc.sync.dma_start(out=ov[b, j], in_=o_sb[b, j][:])
+        def group_in(s, stage):
+            g, rest = divmod(s - GROUP_READY - stage, CHUNKS * PACK)
+            return g if rest == 0 and 0 <= g < GROUPS else -1
 
-        for piece in range(4):
-            w_regroup("gpsimd", 0, piece)
-        for s in range(-5, (NH + 4) * NC):
-            i, k = divmod(s, NC)
-            bg, since = divmod(i - 7, 4)
-            if 0 <= s + 1 < NS:
-                qk_mm(s + 1)
-            if k == 3 and 0 <= i + 2 < NH:
-                tqk(i + 2)
-            if 0 <= i - 3 < NH:
-                if k == 0:
-                    gt(i - 3, 0)
-                if k == 1:
-                    gt(i - 3, 1)
-                    gt(i - 3, 2)
-                if k == 2:
-                    gt(i - 3, 3)
-            if k == 2 and since == 0 and 0 <= bg < 4:
-                ta(bg)
-            if 0 <= s < NS:
-                vmax(s)
-            if k == 2 and 0 <= i - 1 < NH:
-                rc(i - 1)
-                if i - 1 == NH - 1:
-                    sc("vector", i - 1, 0)
-                    sc("vector", i - 1, 2)
-            if k == 3 and 0 <= i - 3 < NH:
-                red(i - 3)
-            if k == 0 and 0 <= i - 4 < NH:
-                av(i - 4)
-            if k == 0 and 0 <= i - 2 < NH - 1:
-                sc("vector", i - 2, 3)
-            if k == 0 and since == 2 and 0 <= bg < 3:
-                qa(bg)
-            if k == 2 and 5 <= i < 7:
-                w_quant(0, i - 5)
-            if k == 2 and 11 <= i < 13:
-                w_quant(1, i - 11)
-            if 0 <= s < NS:
-                nbias(s)
-            if 0 <= s - 1 < NS:
-                expo(s - 1)
-            if k == 0 and 0 <= i + 1 < NH:
-                evq(i + 1)
-            if k == 2 and i - 1 == NH - 1:
-                sc("scalar", i - 1, 1)
-                sc("scalar", i - 1, 3)
-            piece = 4 * since + k - 3
-            if 0 <= bg < 3 and 0 <= piece < 4:
-                eva("scalar", bg, piece // 2, piece % 2)
-            h, c = divmod(s - 6, NC)
-            if 0 <= h < NH - 1 and c < 3:
-                sc("gpsimd", h, c)
-            if 5 <= h < 9 and c == 3:
-                w_regroup("gpsimd", 1, h - 5)
-            if bg == 1 and since == 2 and k == 2:
-                for u in range(8):
-                    mx_group(0, u)
-                    out_group(0, u)
-            if bg == 3 and since == 0 and k == 3:
-                for jj in range(2):
-                    eva("scalar", bg, jj, 0)
-                    eva("vector", bg, jj, 1)
-                    qa_half(bg, jj)
-                for u in range(8):
-                    mx_group(1, u)
-                    out_group(1, u)
+        last = HEADS - 1
+        for quarter in range(4):
+            regroup_w(0, quarter)
+        for s in range(TRANSPOSE_QK, CHUNKS * PACK * (GROUPS - 1) + GROUP_READY + COPY_A + 1):
+            if 0 <= s + 1 < ALL_CHUNKS:
+                scores(s + 1)
+            if head_in(s, TRANSPOSE_QK) >= 0:
+                transpose_qk(head_in(s, TRANSPOSE_QK))
+            for j in range(CHUNKS):
+                if head_in(s, GATE[j]) >= 0:
+                    gate_sum(head_in(s, GATE[j]), j)
+            if group_in(s, TRANSPOSE_A) >= 0:
+                transpose_a(group_in(s, TRANSPOSE_A))
+            if 0 <= s < ALL_CHUNKS:
+                maximum(s)
+            if head_in(s, RECIPROCAL) >= 0:
+                reciprocal(head_in(s, RECIPROCAL))
+            if head_in(s, RECIPROCAL) == last:
+                scale_vector(last, 0)
+                scale_vector(last, 2)
+            if head_in(s, REDUCE) >= 0:
+                reduce_gate(head_in(s, REDUCE))
+            if head_in(s, WEIGH) >= 0:
+                weigh(head_in(s, WEIGH))
+            if 0 <= head_in(s, SCALE_VECTOR) < last:
+                scale_vector(head_in(s, SCALE_VECTOR), 3)
+            if 0 <= group_in(s, QUANTISE_A) < GROUPS - 1:
+                quantise_a(group_in(s, QUANTISE_A), 0)
+                quantise_a(group_in(s, QUANTISE_A), 1)
+            for r in range(PARTS):
+                for half in range(D_OUT // N_MX):
+                    if s == W_QUANTISE[r][half]:
+                        quantise_w(r, half)
+            if 0 <= s < ALL_CHUNKS:
+                exp_bias(s)
+            if 0 <= s - 1 < ALL_CHUNKS:
+                exponentials(s - 1)
+            if head_in(s, COPY_QK) >= 0:
+                copy_qk(head_in(s, COPY_QK))
+            if head_in(s, RECIPROCAL) == last:
+                scale_scalar(last, 1)
+                scale_scalar(last, 3)
+            for j in range(CHUNKS):
+                if 0 <= group_in(s, COPY_A + j) < GROUPS - 1:
+                    copy_a(nc.scalar.copy, group_in(s, COPY_A + j), j)
+            for c in range(3):
+                if 0 <= head_in(s, SCALE_GPSIMD + c) < last:
+                    scale_gpsimd(head_in(s, SCALE_GPSIMD + c), c)
+            if W_LATE_HEAD <= head_in(s, SCALE_GPSIMD + 3) < W_LATE_HEAD + 4:
+                regroup_w(1, head_in(s, SCALE_GPSIMD + 3) - W_LATE_HEAD)
+            if group_in(s, PROJECT) == PARTS - 1:
+                project(0)
+            if group_in(s, COPY_A) == GROUPS - 1:
+                for pair in range(CHUNKS // 2):
+                    copy_a(nc.scalar.copy, GROUPS - 1, 2 * pair)
+                    copy_a(nc.vector.tensor_copy, GROUPS - 1, 2 * pair + 1)
+                    quantise_a(GROUPS - 1, pair)
+                project(BATCHES - 1)

from contextlib import ExitStack
import math

import concourse.masks as masks
import concourse.mybir as mybir

BF16 = mybir.dt.bfloat16
F32 = mybir.dt.float32
U32 = mybir.dt.uint32
U8 = mybir.dt.uint8
FP8X4 = mybir.dt.float8_e4m3fn_x4
ACT = mybir.ActivationFunctionType
ALU = mybir.AluOpType
AX = mybir.AxisListType

P = 128
BATCHES, HEADS_PER_BATCH, TOKENS, D_OUT = 2, 8, 512, 1024
HEADS = BATCHES * HEADS_PER_BATCH
CHUNKS = TOKENS // P
ALL_CHUNKS = HEADS * CHUNKS
PACK = 4
GROUPS = HEADS // PACK
PARTS = GROUPS // BATCHES
N_MX = 512
SCALE = math.sqrt(P)
FLOPS = 2 * HEADS * TOKENS * TOKENS * (P + 1) + 2 * BATCHES * TOKENS * HEADS_PER_BATCH * P * D_OUT

TRANSPOSE_QK = -5
COPY_QK = -4
RECIPROCAL = 6
SCALE_GPSIMD = 6
SCALE_VECTOR = 8
GATE = (12, 13, 13, 14)
REDUCE = 15
WEIGH = 16
GROUP_READY = CHUNKS * (PACK - 1) + WEIGH
TRANSPOSE_A = 2
COPY_A = 3
QUANTISE_A = 8
PROJECT = 10
W_LATE_HEAD = 5
W_QUANTISE = ((22, 26), (46, 50))


def tile_attn_pb_kernel(tc, q_rot, k_rot, v, w_out, b_out, out):
    nc = tc.nc
    with ExitStack() as ctx:
        const = ctx.enter_context(tc.tile_pool(name="const", bufs=1))
        keep = ctx.enter_context(tc.tile_pool(name="keep", bufs=1))
        qk_pool = ctx.enter_context(tc.tile_pool(name="qkt", bufs=4))
        e_pool = ctx.enter_context(tc.tile_pool(name="e", bufs=5))
        st_pool = ctx.enter_context(tc.tile_pool(name="stat", bufs=6))
        a_pool = ctx.enter_context(tc.tile_pool(name="a", bufs=2))
        o_pool = ctx.enter_context(tc.tile_pool(name="o", bufs=6))
        ps_s = ctx.enter_context(tc.psum_pool(name="ps_s", bufs=4))
        ps_t = ctx.enter_context(tc.psum_pool(name="ps_t", bufs=1))
        ps_c = ctx.enter_context(tc.psum_pool(name="ps_c", bufs=1))
        ps_x = ctx.enter_context(tc.psum_pool(name="ps_x", bufs=2))
        ctx.enter_context(tc.manual_schedule())

        q_view = q_rot.rearrange("b h (p c) d -> p (b h) (c d)", c=CHUNKS)
        k_view = k_rot.rearrange("b h (p c) d -> p (b h) (c d)", c=CHUNKS)
        v_view = v.rearrange("b h (p c) d -> p (b h) (c d)", c=CHUNKS)
        w_view = w_out.rearrange("(r t p) n -> p r t n", r=PARTS, t=PACK)
        q_sb, k_sb, v_sb = {}, {}, {}

        def load(dst, view, first, count, label):
            t_in = keep.tile([P, count, TOKENS], BF16, name="%s%d" % (label, first))
            nc.sync.dma_start(out=t_in[:], in_=view[:, first:first + count, :])
            for h in range(count):
                dst[first + h] = t_in[:, h, :]

        w_raw = [keep.tile([P, PACK, D_OUT], BF16, name="wraw%d" % r) for r in range(PARTS)]
        bias_bc = keep.tile([P, D_OUT], BF16, name="bias_bc")
        for h in range(2):
            load(q_sb, q_view, h, 1, "q")
            load(k_sb, k_view, h, 1, "k")
        nc.sync.dma_start(out=w_raw[0][:], in_=w_view[:, 0])
        load(v_sb, v_view, 0, 2, "v")
        load(q_sb, q_view, 2, 2, "q")
        load(k_sb, k_view, 2, 2, "k")
        nc.sync.dma_start(out=w_raw[1][:], in_=w_view[:, 1])
        load(v_sb, v_view, 2, 2, "v")
        nc.sync.dma_start(out=bias_bc[:], in_=b_out.partition_broadcast(P))
        for first in range(4, HEADS, 2):
            load(q_sb, q_view, first, 2, "q")
            load(k_sb, k_view, first, 2, "k")
            load(v_sb, v_view, first, 2, "v")

        ident = const.tile([P, P], BF16, name="ident")
        masks.make_identity(nc, ident[:])
        ident_f = const.tile([P, P], F32, name="ident_f")
        masks.make_identity(nc, ident_f[:])
        warm = const.tile([P, 2], F32, name="warm")
        nc.vector.memset(warm[:], 0.0)
        nc.scalar.activation(out=warm[:, 1:2], in_=warm[:, 0:1], func=ACT.Exp)

        w_grouped = [keep.tile([P, D_OUT, PACK], BF16, name="wgrp%d" % r, align_bytes=64) for r in range(PARTS)]
        w_codes = keep.tile([P, PARTS, D_OUT], U32, name="w_codes", align_bytes=64)
        w_scales = keep.tile([P, PARTS, D_OUT], U8, name="w_scales", align_bytes=64)

        def regroup_w(r, quarter):
            cols = slice(quarter * D_OUT // 4, (quarter + 1) * D_OUT // 4)
            nc.gpsimd.tensor_scalar(out=w_grouped[r][:, cols, :],
                                    in0=w_raw[r][:, :, cols].rearrange("p t n -> p n t"),
                                    scalar1=1.0, scalar2=0.0, op0=ALU.mult, op1=ALU.add)

        def quantise_w(r, half):
            cols = slice(half * N_MX, (half + 1) * N_MX)
            nc.vector.quantize_mx(out=w_codes[:, r, cols].bitcast(FP8X4), scales=w_scales[:, r, cols],
                                  in_=w_grouped[r][:, cols, :].rearrange("p n t -> p (n t)"))

        qk_ps, qk_t, score, expo, gate_ps = {}, {}, {}, {}, {}
        row_max, bias, row_sum, inv_sum, gate = {}, {}, {}, {}, {}

        def transpose_qk(h):
            qk_ps[h] = ps_t.tile([P, 2 * TOKENS], BF16, name="tp")
            for half, src in enumerate((q_sb[h], k_sb[h])):
                for c in range(CHUNKS):
                    nc.tensor.transpose(out=qk_ps[h][:, half * TOKENS + c * P:half * TOKENS + (c + 1) * P],
                                        in_=src[:, c * P:(c + 1) * P], identity=ident[:])

        def copy_qk(h):
            qk_t[h] = qk_pool.tile([P, 2 * TOKENS], BF16, name="qkT")
            nc.scalar.copy(out=qk_t[h][:], in_=qk_ps[h][:])

        def scores(s):
            h, c = divmod(s, CHUNKS)
            score[s] = ps_s.tile([P, TOKENS], F32, name="s_ps", tag="s")
            nc.tensor.matmul(out=score[s][:], lhsT=qk_t[h][:, c * P:(c + 1) * P], rhs=qk_t[h][:, TOKENS:],
                             start=True, stop=True)

        def maximum(s):
            h, c = divmod(s, CHUNKS)
            if c == 0:
                row_max[h] = st_pool.tile([P, CHUNKS], F32, name="mx")
            nc.vector.tensor_reduce(out=row_max[h][:, c:c + 1], in_=score[s][:], axis=AX.X, op=ALU.max)

        def exp_bias(s):
            h, c = divmod(s, CHUNKS)
            if c == 0:
                bias[h] = st_pool.tile([P, CHUNKS], F32, name="nb")
            nc.scalar.mul(out=bias[h][:, c:c + 1], in_=row_max[h][:, c:c + 1], mul=-SCALE)

        def exponentials(s):
            h, c = divmod(s, CHUNKS)
            if c == 0:
                row_sum[h] = st_pool.tile([P, CHUNKS], F32, name="rs")
                expo[h] = e_pool.tile([P, CHUNKS, TOKENS], F32, name="e_t")
            nc.scalar.activation(out=expo[h][:, c, :], in_=score[s][:], func=ACT.Exp,
                                 bias=bias[h][:, c:c + 1], scale=SCALE, accum_out=row_sum[h][:, c:c + 1])

        def reciprocal(h):
            inv_sum[h] = st_pool.tile([P, CHUNKS], F32, name="rr")
            nc.vector.reciprocal(out=inv_sum[h][:], in_=row_sum[h][:])

        def scale_gpsimd(h, c):
            nc.gpsimd.tensor_scalar(out=expo[h][:, c, :], in0=expo[h][:, c, :], scalar1=inv_sum[h][:, c:c + 1],
                                    scalar2=0.0, op0=ALU.mult, op1=ALU.add)

        def scale_vector(h, c):
            nc.vector.tensor_scalar(out=expo[h][:, c, :], in0=expo[h][:, c, :], scalar1=inv_sum[h][:, c:c + 1],
                                    scalar2=None, op0=ALU.mult)

        def scale_scalar(h, c):
            nc.scalar.activation(out=expo[h][:, c, :], in_=expo[h][:, c, :], func=ACT.Copy,
                                 scale=inv_sum[h][:, c:c + 1])

        def gate_sum(h, j):
            if j == 0 and h < HEADS - 2:
                gate_ps[h] = ps_c.tile([P, CHUNKS, P], F32, name="cg")
            if j == 0 and h >= HEADS - 2:
                gate_ps[h] = ps_s.tile([P, CHUNKS, P], F32, name="cg_s", tag="s")
            for c in range(CHUNKS):
                nc.tensor.matmul(out=gate_ps[h][:, j, :], lhsT=expo[h][:, c, j * P:(j + 1) * P], rhs=ident_f[:],
                                 start=(c == 0), stop=(c == CHUNKS - 1), is_transpose=True)

        def reduce_gate(h):
            gate[h] = st_pool.tile([P, CHUNKS], F32, name="cv")
            nc.vector.tensor_reduce(out=gate[h][:], in_=gate_ps[h][:], axis=AX.X, op=ALU.add)

        weighed, a_ps, a_grouped, a_codes, a_scales = {}, {}, {}, {}, {}

        def weigh(h):
            g, t = divmod(h, PACK)
            if t == 0:
                weighed[g] = a_pool.tile([P, PACK, CHUNKS, P], BF16, name="a4")
            for j in range(CHUNKS):
                nc.vector.tensor_scalar(out=weighed[g][:, t, j, :], in0=v_sb[h][:, j * P:(j + 1) * P],
                                        scalar1=gate[h][:, j:j + 1], scalar2=None, op0=ALU.mult)

        def transpose_a(g):
            for pair in range(CHUNKS // 2):
                a_ps[g, pair] = ps_x.tile([P, PACK, 2 * P], BF16, name="ta_x", tag="x")
            for t in range(PACK):
                for j in range(CHUNKS):
                    nc.tensor.transpose(out=a_ps[g, j // 2][:, t, (j % 2) * P:(j % 2 + 1) * P],
                                        in_=weighed[g][:, t, j, :], identity=ident[:])

        def copy_a(copy, g, j):
            if j == 0:
                a_grouped[g] = a_pool.tile([P, CHUNKS, P, PACK], BF16, name="grp", align_bytes=64)
            copy(out=a_grouped[g][:, j, :, :],
                 in_=a_ps[g, j // 2][:, :, (j % 2) * P:(j % 2 + 1) * P].rearrange("p t x -> p x t"))

        def quantise_a(g, pair):
            if pair == 0:
                a_codes[g] = keep.tile([P, TOKENS], U32, name="a_codes%d" % g, align_bytes=64)
                a_scales[g] = keep.tile([P, TOKENS], U8, name="a_scales%d" % g, align_bytes=64)
            cols = slice(pair * 2 * P, (pair + 1) * 2 * P)
            nc.vector.quantize_mx(out=a_codes[g][:, cols].bitcast(FP8X4), scales=a_scales[g][:, cols],
                                  in_=a_grouped[g][:, 2 * pair:2 * pair + 2].rearrange("p j x t -> p (j x t)"))

        out_view = out.rearrange("b (p j) n -> b j p n", j=CHUNKS)

        def project(b):
            for j in range(CHUNKS):
                for half in range(D_OUT // N_MX):
                    cols = slice(half * N_MX, (half + 1) * N_MX)
                    if b == BATCHES - 1:
                        acc = ps_s.tile([P, N_MX], F32, name="o_s", tag="s")
                    else:
                        acc = ps_x.tile([P, N_MX], F32, name="o_x", tag="x")
                    for r in range(PARTS):
                        g = PARTS * b + r
                        nc.tensor.matmul_mx(out=acc[:],
                                            lhsT=a_codes[g][:, j * P:(j + 1) * P].bitcast(FP8X4),
                                            lhsT_scale=a_scales[g][:, j * P:(j + 1) * P],
                                            rhs=w_codes[:, r, cols].bitcast(FP8X4), rhs_scale=w_scales[:, r, cols],
                                            start=(r == 0), stop=(r == PARTS - 1))
                    o_sb = o_pool.tile([P, N_MX], F32, name="o_sb")
                    nc.vector.tensor_tensor(out=o_sb[:], in0=acc[:], in1=bias_bc[:, cols], op=ALU.add)
                    nc.sync.dma_start(out=out_view[b, j][:, cols], in_=o_sb[:])

        def head_in(s, stage):
            h, rest = divmod(s - stage, CHUNKS)
            return h if rest == 0 and 0 <= h < HEADS else -1

        def group_in(s, stage):
            g, rest = divmod(s - GROUP_READY - stage, CHUNKS * PACK)
            return g if rest == 0 and 0 <= g < GROUPS else -1

        last = HEADS - 1
        for quarter in range(4):
            regroup_w(0, quarter)
        for s in range(TRANSPOSE_QK, CHUNKS * PACK * (GROUPS - 1) + GROUP_READY + COPY_A + 1):
            if 0 <= s + 1 < ALL_CHUNKS:
                scores(s + 1)
            if head_in(s, TRANSPOSE_QK) >= 0:
                transpose_qk(head_in(s, TRANSPOSE_QK))
            for j in range(CHUNKS):
                if head_in(s, GATE[j]) >= 0:
                    gate_sum(head_in(s, GATE[j]), j)
            if group_in(s, TRANSPOSE_A) >= 0:
                transpose_a(group_in(s, TRANSPOSE_A))
            if 0 <= s < ALL_CHUNKS:
                maximum(s)
            if head_in(s, RECIPROCAL) >= 0:
                reciprocal(head_in(s, RECIPROCAL))
            if head_in(s, RECIPROCAL) == last:
                scale_vector(last, 0)
                scale_vector(last, 2)
            if head_in(s, REDUCE) >= 0:
                reduce_gate(head_in(s, REDUCE))
            if head_in(s, WEIGH) >= 0:
                weigh(head_in(s, WEIGH))
            if 0 <= head_in(s, SCALE_VECTOR) < last:
                scale_vector(head_in(s, SCALE_VECTOR), 3)
            if 0 <= group_in(s, QUANTISE_A) < GROUPS - 1:
                quantise_a(group_in(s, QUANTISE_A), 0)
                quantise_a(group_in(s, QUANTISE_A), 1)
            for r in range(PARTS):
                for half in range(D_OUT // N_MX):
                    if s == W_QUANTISE[r][half]:
                        quantise_w(r, half)
            if 0 <= s < ALL_CHUNKS:
                exp_bias(s)
            if 0 <= s - 1 < ALL_CHUNKS:
                exponentials(s - 1)
            if head_in(s, COPY_QK) >= 0:
                copy_qk(head_in(s, COPY_QK))
            if head_in(s, RECIPROCAL) == last:
                scale_scalar(last, 1)
                scale_scalar(last, 3)
            for j in range(CHUNKS):
                if 0 <= group_in(s, COPY_A + j) < GROUPS - 1:
                    copy_a(nc.scalar.copy, group_in(s, COPY_A + j), j)
            for c in range(3):
                if 0 <= head_in(s, SCALE_GPSIMD + c) < last:
                    scale_gpsimd(head_in(s, SCALE_GPSIMD + c), c)
            if W_LATE_HEAD <= head_in(s, SCALE_GPSIMD + 3) < W_LATE_HEAD + 4:
                regroup_w(1, head_in(s, SCALE_GPSIMD + 3) - W_LATE_HEAD)
            if group_in(s, PROJECT) == PARTS - 1:
                project(0)
            if group_in(s, COPY_A) == GROUPS - 1:
                for pair in range(CHUNKS // 2):
                    copy_a(nc.scalar.copy, GROUPS - 1, 2 * pair)
                    copy_a(nc.vector.tensor_copy, GROUPS - 1, 2 * pair + 1)
                    quantise_a(GROUPS - 1, pair)
                project(BATCHES - 1)
